import numpy as np
import ml_dtypes


def mxq(x, axis, fmt="e4m3"):
    dtype, down = {"e4m3": (ml_dtypes.float8_e4m3fn, 7), "e5m2": (ml_dtypes.float8_e5m2, 14)}[fmt]
    v = np.moveaxis(np.asarray(x, np.float32).astype(ml_dtypes.bfloat16).astype(np.float64), axis, -1)
    blocks = v.reshape(v.shape[:-1] + (-1, 32))
    amax = np.abs(blocks).max(-1, keepdims=True)
    byte = np.maximum(np.where(amax > 0, np.frexp(amax)[1] - 1 + 127, 0) - down, 1)
    scale = np.exp2(byte - 127.0)
    codes = (blocks / scale).astype(np.float32).astype(dtype).astype(np.float64)
    return np.moveaxis((codes * scale).reshape(v.shape), -1, axis)


WIDE = False


def mx_kscale(k):
    if not WIDE:
        return np.ones(k)
    levels = np.array([10, -10, 5, -5, 0])
    if k % 512:
        return np.exp2(np.random.permutation(np.resize(levels, k // 32))).repeat(32)
    a = np.empty((k // 512, 16))
    for p in range(k // 512):
        a[p, :8] = np.random.permutation(np.resize(levels, 8))
        for g in range(8):
            far = levels[np.abs(levels - a[p, g]) >= 10]
            a[p, g + 8] = far[np.random.randint(len(far))]
    return np.exp2(a.ravel()).repeat(32)


BF16 = ml_dtypes.bfloat16


def bf(x):
    return np.asarray(x, np.float32).astype(BF16)


def f64(x):
    return np.asarray(x).astype(np.float64)


B, N, T, D, DO, H, E = 128, 2, 8, 512, 512, 8, 128
S = N * T


def sigmoid(v):
    return 1.0 / (1.0 + np.exp(-v))


def setup_inputs():
    r = np.random.standard_normal
    s = mx_kscale(D)
    return {
        "x": bf(r((B, S, D)) * s),
        "edge_features": bf(r((B, E))),
        "Wv": bf(r((D, DO)) / np.sqrt(D) / s[:, None]),
        "bv": bf(r(DO) * 0.3),
        "Wgate": bf(r((E, DO)) / np.sqrt(E)),
        "bgate": bf(r(DO) * 0.3),
        "Wscale": bf(r((E, DO)) * 0.7 / np.sqrt(E)),
        "bscale": bf(r(DO) * 0.3),
        "Wshift": bf(r((E, DO)) * 0.7 / np.sqrt(E)),
        "bshift": bf(r(DO) * 0.3),
    }


def core(x, edge_features, Wv, bv, Wgate, bgate, Wscale, bscale, Wshift, bshift):
    e = f64(edge_features)
    v = (mxq(f64(x).reshape(B * S, D), 1, "e4m3") @ mxq(f64(Wv), 0, "e4m3")).reshape(B, S, DO) + f64(bv)
    gate = sigmoid(e @ f64(Wgate) + f64(bgate))
    scale = np.tanh(e @ f64(Wscale) + f64(bscale))
    shift = e @ f64(Wshift) + f64(bshift)
    return (v * (1.0 + scale[:, None, :]) + shift[:, None, :]) * gate[:, None, :]


def e4m3fn_bytes(y):
    return np.clip(np.asarray(y, np.float64), -448.0, 448.0).astype(np.float32).astype(ml_dtypes.float8_e4m3fn).view(np.uint8)


def reference(x, edge_features, Wv, bv, Wgate, bgate, Wscale, bscale, Wshift, bshift):
    out = core(x, edge_features, Wv, bv, Wgate, bgate, Wscale, bscale, Wshift, bshift)
    s = np.max(np.abs(out), axis=-1, keepdims=True) / 448.0
    return out, e4m3fn_bytes(out / s)

@@ -1,0 +1,296 @@
+from contextlib import ExitStack
+
+import concourse.mybir as mybir
+from concourse.masks import make_identity
+
+F32 = mybir.dt.float32
+BF16 = mybir.dt.bfloat16
+U32 = mybir.dt.uint32
+U8 = mybir.dt.uint8
+FP8X4 = mybir.dt.float8_e4m3fn_x4
+FP8 = mybir.dt.float8_e4m3fn
+ALU = mybir.AluOpType
+ACT = mybir.ActivationFunctionType
+AX = mybir.AxisListType
+
+P = 128
+ROWS = 16
+D = 512
+DO = 512
+FLOPS = 2 * 2048 * 512 * 512 + 3 * 2 * 128 * 128 * 512
+
+X_AHEAD = 4
+STORE_GROUPS = ((0, 4), (4, 4), (8, 4), (12, 2), (14, 2))
+
+
+def tile_graphditunit_pa_kernel(
+    tc, x, edge_features, Wv, bv, Wgate, bgate, Wscale, bscale, Wshift, bshift, out_0, out_1
+):
+    nc = tc.nc
+    n_pairs = ROWS // 2
+
+    with ExitStack() as ctx:
+        const = ctx.enter_context(tc.tile_pool(name="const", bufs=1))
+        work = ctx.enter_context(tc.tile_pool(name="work", bufs=3))
+        psum = ctx.enter_context(tc.psum_pool(name="psum", bufs=8))
+        ctx.enter_context(tc.manual_schedule())
+
+        def bank(shape, dtype, name):
+            return psum.tile(shape, dtype, name=name, tag="bank", bufs=8)
+
+        zeros = const.tile([P, 1], F32, name="zeros")
+        nc.gpsimd.memset(zeros[:], 0.0)
+        warm = const.tile([P, 1], F32, name="warm")
+        nc.scalar.activation(out=warm[:], in_=zeros[:], func=ACT.Sigmoid)
+        biasrows = const.tile([P, DO], BF16, name="biasrows")
+        nc.gpsimd.memset(biasrows[:], 0.0)
+        ident_bf = const.tile([P, P], BF16, name="ident_bf")
+        make_identity(nc, ident_bf[:])
+        ident_f = const.tile([P, P], F32, name="ident_f")
+        make_identity(nc, ident_f[:])
+
+        e_sb = const.tile([P, P], BF16, name="e_sb")
+        nc.sync.dma_start(out=e_sb[:], in_=edge_features)
+        ws_sb = const.tile([P, DO], BF16, name="ws_sb")
+        nc.sync.dma_start(out=ws_sb[:], in_=Wscale)
+        wg_sb = const.tile([P, DO], BF16, name="wg_sb")
+        nc.sync.dma_start(out=wg_sb[:], in_=Wgate)
+        for j, b in enumerate((bscale, bgate, bshift, bv)):
+            nc.sync.dma_start(out=biasrows[j : j + 1, :], in_=b.rearrange("(o n) -> o n", o=1))
+        w_raw = []
+        for h in range(2):
+            wr = const.tile([P, 4, DO // 2], BF16, name="w_raw%d" % h)
+            nc.sync.dma_start(out=wr[:], in_=Wv[:, 256 * h : 256 * (h + 1)].rearrange("(p j) c -> p j c", j=4))
+            w_raw.append(wr)
+        wh_sb = const.tile([P, DO], BF16, name="wh_sb")
+        nc.sync.dma_start(out=wh_sb[:], in_=Wshift)
+        x_sb = []
+        for c in range(n_pairs):
+            x_sb.append(const.tile([P, 2, D], BF16, name="x_sb%d" % c))
+        nc.sync.dma_start(out=x_sb[0][:], in_=x[:, 0:2, :])
+        for c in range(1, n_pairs):
+            nc.sync.dma_start(out=x_sb[c][:], in_=x[:, 2 * c : 2 * c + 2, :])
+
+        x_codes = {}
+        x_scales = {}
+        xg_tiles = {}
+
+        def x_transpose(c):
+            words = x_sb[c][:].rearrange("p t k -> p (t k)").bitcast(F32)
+            xt = bank([P, 2, 2, P], F32, "xt")
+            for t in range(2):
+                for u in range(2):
+                    nc.tensor.transpose(xt[:, t, u, :], words[:, 256 * t + u : 256 * (t + 1) : 2], ident_f[:])
+            xg = work.tile([P, 2, P, 2], F32, name="xg", tag="xg", bufs=8, align_bytes=64)
+            nc.scalar.copy(out=xg[:], in_=xt[:].rearrange("p t u r -> p t r u"))
+            xg_tiles[c] = xg
+
+        def x_quantise(c):
+            xc = const.tile([P, 2 * P], U32, name="xc%d" % c, align_bytes=64)
+            xs = const.tile([P, 2 * P], U8, name="xs%d" % c, align_bytes=64)
+            nc.vector.quantize_mx(
+                out=xc[:].bitcast(FP8X4),
+                scales=xs[:],
+                in_=xg_tiles[c][:].rearrange("p t r u -> p (t r u)").bitcast(BF16),
+            )
+            x_codes[c] = xc
+            x_scales[c] = xs
+
+        selm = const.tile([P, 3, P], BF16, name="selm")
+        nc.vector.tensor_copy(out=selm[:, 0:2, :], in_=ident_bf[:, 0:2].unsqueeze(2).to_broadcast([P, 2, P]))
+        nc.vector.tensor_tensor(
+            out=selm[:, 2, :],
+            in0=ident_bf[:, 2:3].to_broadcast([P, P]),
+            in1=ident_bf[:, 3:4].to_broadcast([P, P]),
+            op=ALU.add,
+        )
+
+        eT_ps = bank([P, P], BF16, "eT_ps")
+        nc.tensor.transpose(eT_ps[:], e_sb[:], ident_bf[:])
+        eT = const.tile([P, P], BF16, name="eT")
+        nc.scalar.copy(out=eT[:], in_=eT_ps[:])
+
+        def modulation(w, v, name):
+            zT = bank([P, 4, P], F32, name)
+            for j in range(4):
+                cols = slice(P * j, P * (j + 1))
+                nc.tensor.matmul(out=zT[:, j, :], lhsT=w[:, cols], rhs=eT[:], start=True, stop=False)
+                nc.tensor.matmul(out=zT[:, j, :], lhsT=biasrows[:, cols], rhs=selm[:, v, :], start=False, stop=True)
+            return zT
+
+        z_s = modulation(ws_sb, 0, "z_s")
+        sT = const.tile([P, 4, P], F32, name="sT")
+        nc.scalar.activation(out=sT[:], in_=z_s[:], func=ACT.Tanh)
+        z_g = modulation(wg_sb, 1, "z_g")
+        gT = const.tile([P, 4, P], F32, name="gT")
+        nc.scalar.activation(out=gT[:], in_=z_g[:], func=ACT.Sigmoid)
+
+        bT_ps = bank([P, 4, P], BF16, "bT_ps")
+        for j in range(4):
+            nc.tensor.transpose(bT_ps[:, j, :], biasrows[:, P * j : P * (j + 1)], ident_bf[:])
+        bvcol = const.tile([P, 4], F32, name="bvcol")
+        nc.scalar.copy(out=bvcol[:], in_=bT_ps[:, :, 3])
+        z_h = modulation(wh_sb, 2, "z_h")
+
+        w_grp = const.tile([P, DO, 4], BF16, name="w_grp", align_bytes=64)
+        for h in range(2):
+            nc.vector.tensor_copy(
+                out=w_grp[:, 256 * h : 256 * (h + 1), :], in_=w_raw[h][:].rearrange("p j c -> p c j")
+            )
+        w_codes = const.tile([P, DO], U32, name="w_codes", align_bytes=64)
+        w_scales = const.tile([P, DO], U8, name="w_scales", align_bytes=64)
+        nc.vector.quantize_mx(
+            out=w_codes[:].bitcast(FP8X4), scales=w_scales[:], in_=w_grp[:].rearrange("p c j -> p (c j)")
+        )
+
+        aT = const.tile([P, 4, P], F32, name="aT")
+        nc.vector.scalar_tensor_tensor(out=aT[:], in0=sT[:], scalar=1.0, in1=gT[:], op0=ALU.add, op1=ALU.mult)
+        u2 = const.tile([P, 4, P], F32, name="u2")
+        for j in range(4):
+            nc.vector.scalar_tensor_tensor(
+                out=u2[:, j, :],
+                in0=sT[:, j, :],
+                scalar=bvcol[:, j : j + 1],
+                in1=z_h[:, j, :],
+                op0=ALU.mult,
+                op1=ALU.add,
+            )
+        cT = const.tile([P, 4, P], F32, name="cT")
+        nc.gpsimd.tensor_tensor(out=cT[:], in0=u2[:], in1=gT[:], op=ALU.mult)
+
+        amax = const.tile([P, ROWS], F32, name="amax")
+        rec = const.tile([P, ROWS], F32, name="rec")
+        fac = const.tile([P, ROWS], F32, name="fac")
+        facv = const.tile([P, ROWS], F32, name="facv")
+        acc_tiles = {}
+        o_tiles = {}
+        p_tiles = {}
+        q_tiles = {}
+        group_of = {}
+        for first, count in STORE_GROUPS:
+            for i in range(first, first + count):
+                group_of[i] = (first, count)
+
+        def cast_and_store(i, on_vector, factor):
+            first, count = group_of[i]
+            if i == first:
+                q_tiles[first] = work.tile([P, count, DO], FP8, name="q", tag="q", bufs=3)
+            qt = q_tiles[first]
+            src = o_tiles[i // 2][:, i % 2, :]
+            if on_vector:
+                nc.vector.tensor_scalar(
+                    out=qt[:, i - first, :],
+                    in0=src,
+                    scalar1=factor[:, i : i + 1],
+                    scalar2=None,
+                    op0=ALU.mult,
+                    saturate=False,
+                )
+            else:
+                nc.scalar.activation(
+                    out=qt[:, i - first, :],
+                    in_=src,
+                    func=ACT.Identity,
+                    bias=zeros[:, 0:1],
+                    scale=factor[:, i : i + 1],
+                    saturate=False,
+                )
+            if i == first + count - 1:
+                nc.sync.dma_start(out=out_1[:, first : first + count, :], in_=qt[:].bitcast(U8))
+
+        def mx_pair(c):
+            for t in range(2):
+                accT = bank([P, 4, P], F32, "accT")
+                acc_tiles[2 * c + t] = accT
+                rows = slice(P * t, P * (t + 1))
+                for j in range(4):
+                    cols = slice(P * j, P * (j + 1))
+                    nc.tensor.matmul_mx(
+                        out=accT[:, j, :],
+                        lhsT=w_codes[:, cols].bitcast(FP8X4),
+                        lhsT_scale=w_scales[:, cols],
+                        rhs=x_codes[c][:, rows].bitcast(FP8X4),
+                        rhs_scale=x_scales[c][:, rows],
+                        start=True,
+                        stop=True,
+                    )
+
+        def times_a(i):
+            prodT = work.tile([P, 4, P], F32, name="prodT", tag="prodT", bufs=4)
+            p_tiles[i] = prodT
+            nc.vector.tensor_tensor(out=prodT[:], in0=acc_tiles[i][:], in1=aT[:], op=ALU.mult)
+
+        def turn_back(i, store_now):
+            if i % 2 == 0:
+                o_tiles[i // 2] = work.tile([P, 2, DO], F32, name="o", tag="o", bufs=5)
+            o = o_tiles[i // 2]
+            o_ps = bank([P, DO], F32, "o_ps")
+            for j in range(4):
+                cols = slice(P * j, P * (j + 1))
+                nc.tensor.matmul(
+                    out=o_ps[:, cols], lhsT=cT[:, j, :], rhs=ident_f[:], start=True, stop=False, is_transpose=True
+                )
+                nc.tensor.matmul(
+                    out=o_ps[:, cols], lhsT=p_tiles[i][:, j, :], rhs=ident_f[:], start=False, stop=True, is_transpose=True
+                )
+            nc.scalar.copy(out=o[:, i % 2, :], in_=o_ps[:])
+            if store_now:
+                nc.sync.dma_start(out=out_0[:, i : i + 1, :], in_=o[:, i % 2 : i % 2 + 1, :])
+            elif i % 2 == 1:
+                nc.sync.dma_start(out=out_0[:, i - 1 : i + 1, :], in_=o[:])
+
+        def row_factors_pair(c):
+            cols = slice(2 * c, 2 * c + 2)
+            nc.vector.tensor_reduce(
+                out=amax[:, cols], in_=o_tiles[c][:], axis=AX.X, op=ALU.max, apply_absolute_value=True
+            )
+            nc.vector.reciprocal(out=rec[:, cols], in_=amax[:, cols])
+            nc.gpsimd.tensor_scalar(
+                out=fac[:, cols], in0=rec[:, cols], scalar1=448.0, scalar2=0.0, op0=ALU.mult, op1=ALU.add
+            )
+
+        def row_factor_tile(i):
+            nc.vector.tensor_reduce(
+                out=amax[:, i : i + 1],
+                in_=o_tiles[i // 2][:, i % 2, :],
+                axis=AX.X,
+                op=ALU.max,
+                apply_absolute_value=True,
+            )
+            nc.vector.reciprocal(out=rec[:, i : i + 1], in_=amax[:, i : i + 1])
+            nc.vector.tensor_scalar(
+                out=facv[:, i : i + 1], in0=rec[:, i : i + 1], scalar1=448.0, scalar2=None, op0=ALU.mult
+            )
+
+        x_transpose(0)
+        x_quantise(0)
+        x_transpose(1)
+        x_quantise(1)
+        for c in range(2, X_AHEAD):
+            x_transpose(c)
+        mx_pair(0)
+
+        for k in range(n_pairs):
+            last = k == n_pairs - 1
+            if not last:
+                mx_pair(k + 1)
+            times_a(2 * k)
+            times_a(2 * k + 1)
+            if k >= 2:
+                cast_and_store(2 * k - 4, False, fac)
+                cast_and_store(2 * k - 3, False, fac)
+            turn_back(2 * k, last)
+            turn_back(2 * k + 1, last)
+            if k + X_AHEAD < n_pairs:
+                x_transpose(k + X_AHEAD)
+            if k + 2 < n_pairs:
+                x_quantise(k + 2)
+            if k >= 1:
+                row_factors_pair(k - 1)
+
+        cast_and_store(ROWS - 4, False, fac)
+        row_factor_tile(ROWS - 2)
+        cast_and_store(ROWS - 3, False, fac)
+        row_factor_tile(ROWS - 1)
+        cast_and_store(ROWS - 2, False, facv)
+        cast_and_store(ROWS - 1, True, facv)

@@ -48,6 +48,8 @@ def tile_graphditunit_pa_kernel(
         make_identity(nc, ident_bf[:])
         ident_f = const.tile([P, P], F32, name="ident_f")
         make_identity(nc, ident_f[:])
+        minus_one = const.tile([P, ROWS], F32, name="minus_one")
+        nc.gpsimd.memset(minus_one[:], -1.0)
 
         e_sb = const.tile([P, P], BF16, name="e_sb")
         nc.sync.dma_start(out=e_sb[:], in_=edge_features)
@@ -160,6 +162,7 @@ def tile_graphditunit_pa_kernel(
 
         amax = const.tile([P, ROWS], F32, name="amax")
         rec = const.tile([P, ROWS], F32, name="rec")
+        recv = const.tile([P, ROWS], F32, name="recv")
         fac = const.tile([P, ROWS], F32, name="fac")
         facv = const.tile([P, ROWS], F32, name="facv")
         acc_tiles = {}
@@ -244,7 +247,7 @@ def tile_graphditunit_pa_kernel(
             nc.vector.tensor_reduce(
                 out=amax[:, cols], in_=o_tiles[c][:], axis=AX.X, op=ALU.max, apply_absolute_value=True
             )
-            nc.vector.reciprocal(out=rec[:, cols], in_=amax[:, cols])
+            nc.gpsimd.tensor_tensor(out=rec[:, cols], in0=amax[:, cols], in1=minus_one[:, cols], op=ALU.pow)
             nc.gpsimd.tensor_scalar(
                 out=fac[:, cols], in0=rec[:, cols], scalar1=448.0, scalar2=0.0, op0=ALU.mult, op1=ALU.add
             )
@@ -257,9 +260,9 @@ def tile_graphditunit_pa_kernel(
                 op=ALU.max,
                 apply_absolute_value=True,
             )
-            nc.vector.reciprocal(out=rec[:, i : i + 1], in_=amax[:, i : i + 1])
+            nc.vector.reciprocal(out=recv[:, i : i + 1], in_=amax[:, i : i + 1])
             nc.vector.tensor_scalar(
-                out=facv[:, i : i + 1], in0=rec[:, i : i + 1], scalar1=448.0, scalar2=None, op0=ALU.mult
+                out=facv[:, i : i + 1], in0=recv[:, i : i + 1], scalar1=448.0, scalar2=None, op0=ALU.mult
             )
 
         x_transpose(0)

@@ -98,41 +98,38 @@ def tile_graphditunit_pa_kernel(
             x_codes[c] = xc
             x_scales[c] = xs
 
-        selm = const.tile([P, 3, P], BF16, name="selm")
-        nc.vector.tensor_copy(out=selm[:, 0:2, :], in_=ident_bf[:, 0:2].unsqueeze(2).to_broadcast([P, 2, P]))
-        nc.vector.tensor_tensor(
-            out=selm[:, 2, :],
-            in0=ident_bf[:, 2:3].to_broadcast([P, P]),
-            in1=ident_bf[:, 3:4].to_broadcast([P, P]),
-            op=ALU.add,
-        )
-
         eT_ps = bank([P, P], BF16, "eT_ps")
         nc.tensor.transpose(eT_ps[:], e_sb[:], ident_bf[:])
         eT = const.tile([P, P], BF16, name="eT")
         nc.scalar.copy(out=eT[:], in_=eT_ps[:])
 
-        def modulation(w, v, name):
+        def modulation(w, name):
             zT = bank([P, 4, P], F32, name)
             for j in range(4):
-                cols = slice(P * j, P * (j + 1))
-                nc.tensor.matmul(out=zT[:, j, :], lhsT=w[:, cols], rhs=eT[:], start=True, stop=False)
-                nc.tensor.matmul(out=zT[:, j, :], lhsT=biasrows[:, cols], rhs=selm[:, v, :], start=False, stop=True)
+                nc.tensor.matmul(out=zT[:, j, :], lhsT=w[:, P * j : P * (j + 1)], rhs=eT[:], start=True, stop=True)
             return zT
 
-        z_s = modulation(ws_sb, 0, "z_s")
-        sT = const.tile([P, 4, P], F32, name="sT")
-        nc.scalar.activation(out=sT[:], in_=z_s[:], func=ACT.Tanh)
-        z_g = modulation(wg_sb, 1, "z_g")
-        gT = const.tile([P, 4, P], F32, name="gT")
-        nc.scalar.activation(out=gT[:], in_=z_g[:], func=ACT.Sigmoid)
-
+        z_s = modulation(ws_sb, "z_s")
+        z_g = modulation(wg_sb, "z_g")
         bT_ps = bank([P, 4, P], BF16, "bT_ps")
         for j in range(4):
             nc.tensor.transpose(bT_ps[:, j, :], biasrows[:, P * j : P * (j + 1)], ident_bf[:])
-        bvcol = const.tile([P, 4], F32, name="bvcol")
-        nc.scalar.copy(out=bvcol[:], in_=bT_ps[:, :, 3])
-        z_h = modulation(wh_sb, 2, "z_h")
+        bcols = const.tile([P, 4, 4], F32, name="bcols")
+        nc.scalar.copy(out=bcols[:], in_=bT_ps[:, :, 0:4])
+        bhv = const.tile([P, 4], F32, name="bhv")
+        nc.gpsimd.tensor_tensor(out=bhv[:], in0=bcols[:, :, 2], in1=bcols[:, :, 3], op=ALU.add)
+        sT = const.tile([P, 4, P], F32, name="sT")
+        for j in range(4):
+            nc.scalar.activation(out=sT[:, j, :], in_=z_s[:, j, :], func=ACT.Tanh, bias=bcols[:, j, 0:1])
+        gT = const.tile([P, 4, P], F32, name="gT")
+        for j in range(4):
+            nc.scalar.activation(out=gT[:, j, :], in_=z_g[:, j, :], func=ACT.Sigmoid, bias=bcols[:, j, 1:2])
+        sbv = const.tile([P, 4, P], F32, name="sbv")
+        for j in range(4):
+            nc.scalar.activation(
+                out=sbv[:, j, :], in_=sT[:, j, :], func=ACT.Identity, scale=bcols[:, j, 3:4], bias=bhv[:, j : j + 1]
+            )
+        z_h = modulation(wh_sb, "z_h")
 
         w_grp = const.tile([P, DO, 4], BF16, name="w_grp", align_bytes=64)
         for h in range(2):
@@ -148,15 +145,7 @@ def tile_graphditunit_pa_kernel(
         aT = const.tile([P, 4, P], F32, name="aT")
         nc.vector.scalar_tensor_tensor(out=aT[:], in0=sT[:], scalar=1.0, in1=gT[:], op0=ALU.add, op1=ALU.mult)
         u2 = const.tile([P, 4, P], F32, name="u2")
-        for j in range(4):
-            nc.vector.scalar_tensor_tensor(
-                out=u2[:, j, :],
-                in0=sT[:, j, :],
-                scalar=bvcol[:, j : j + 1],
-                in1=z_h[:, j, :],
-                op0=ALU.mult,
-                op1=ALU.add,
-            )
+        nc.vector.tensor_tensor(out=u2[:], in0=z_h[:], in1=sbv[:], op=ALU.add)
         cT = const.tile([P, 4, P], F32, name="cT")
         nc.gpsimd.tensor_tensor(out=cT[:], in0=u2[:], in1=gT[:], op=ALU.mult)
 

@@ -20,6 +20,7 @@ DO = 512
 FLOPS = 2 * 2048 * 512 * 512 + 3 * 2 * 128 * 128 * 512
 
 X_AHEAD = 4
+WARM_MATMULS = 3
 STORE_GROUPS = ((0, 4), (4, 4), (8, 4), (12, 2), (14, 2))
 
 
@@ -114,6 +115,9 @@ def tile_graphditunit_pa_kernel(
         bT_ps = bank([P, 4, P], BF16, "bT_ps")
         for j in range(4):
             nc.tensor.transpose(bT_ps[:, j, :], biasrows[:, P * j : P * (j + 1)], ident_bf[:])
+        warm_ps = bank([P, DO], F32, "warm_ps")
+        for n in range(WARM_MATMULS):
+            nc.tensor.matmul(out=warm_ps[:], lhsT=ident_bf[:], rhs=ws_sb[:], start=True, stop=True)
         bcols = const.tile([P, 4, 4], F32, name="bcols")
         nc.scalar.copy(out=bcols[:], in_=bT_ps[:, :, 0:4])
         bhv = const.tile([P, 4], F32, name="bhv")

@@ -258,12 +258,17 @@ def tile_graphditunit_pa_kernel(
                 out=facv[:, i : i + 1], in0=recv[:, i : i + 1], scalar1=448.0, scalar2=None, op0=ALU.mult
             )
 
+        def keep_warm():
+            nc.tensor.matmul(out=warm_ps[:, 0:P], lhsT=ident_f[:], rhs=ident_f[:], start=True, stop=True)
+
         x_transpose(0)
         x_quantise(0)
         x_transpose(1)
         x_quantise(1)
+        keep_warm()
         for c in range(2, X_AHEAD):
             x_transpose(c)
+        keep_warm()
         mx_pair(0)
 
         for k in range(n_pairs):

@@ -20,7 +20,6 @@ DO = 512
 FLOPS = 2 * 2048 * 512 * 512 + 3 * 2 * 128 * 128 * 512
 
 X_AHEAD = 4
-WARM_MATMULS = 3
 STORE_GROUPS = ((0, 4), (4, 4), (8, 4), (12, 2), (14, 2))
 
 
@@ -43,8 +42,10 @@ def tile_graphditunit_pa_kernel(
         nc.gpsimd.memset(zeros[:], 0.0)
         warm = const.tile([P, 1], F32, name="warm")
         nc.scalar.activation(out=warm[:], in_=zeros[:], func=ACT.Sigmoid)
+        ones = const.tile([P, DO], BF16, name="ones")
+        nc.vector.memset(ones[:].bitcast(U32), 0x3F803F80)
         biasrows = const.tile([P, DO], BF16, name="biasrows")
-        nc.gpsimd.memset(biasrows[:], 0.0)
+        nc.gpsimd.memset(biasrows[:].bitcast(U32), 0)
         ident_bf = const.tile([P, P], BF16, name="ident_bf")
         make_identity(nc, ident_bf[:])
         ident_f = const.tile([P, P], F32, name="ident_f")
@@ -56,10 +57,10 @@ def tile_graphditunit_pa_kernel(
         nc.sync.dma_start(out=e_sb[:], in_=edge_features)
         ws_sb = const.tile([P, DO], BF16, name="ws_sb")
         nc.sync.dma_start(out=ws_sb[:], in_=Wscale)
-        wg_sb = const.tile([P, DO], BF16, name="wg_sb")
-        nc.sync.dma_start(out=wg_sb[:], in_=Wgate)
         for j, b in enumerate((bscale, bgate, bshift, bv)):
             nc.sync.dma_start(out=biasrows[j : j + 1, :], in_=b.rearrange("(o n) -> o n", o=1))
+        wg_sb = const.tile([P, DO], BF16, name="wg_sb")
+        nc.sync.dma_start(out=wg_sb[:], in_=Wgate)
         w_raw = []
         for h in range(2):
             wr = const.tile([P, 4, DO // 2], BF16, name="w_raw%d" % h)
@@ -70,8 +71,7 @@ def tile_graphditunit_pa_kernel(
         x_sb = []
         for c in range(n_pairs):
             x_sb.append(const.tile([P, 2, D], BF16, name="x_sb%d" % c))
-        nc.sync.dma_start(out=x_sb[0][:], in_=x[:, 0:2, :])
-        for c in range(1, n_pairs):
+        for c in range(n_pairs):
             nc.sync.dma_start(out=x_sb[c][:], in_=x[:, 2 * c : 2 * c + 2, :])
 
         x_codes = {}
@@ -99,10 +99,25 @@ def tile_graphditunit_pa_kernel(
             x_codes[c] = xc
             x_scales[c] = xs
 
+        warm_ps = bank([P, DO], F32, "warm_ps")
+
+        def warm_up():
+            nc.tensor.matmul(out=warm_ps[:], lhsT=ones[:, 0:P], rhs=ones[:], start=True, stop=True)
+
+        warm_up()
+        warm_up()
         eT_ps = bank([P, P], BF16, "eT_ps")
         nc.tensor.transpose(eT_ps[:], e_sb[:], ident_bf[:])
         eT = const.tile([P, P], BF16, name="eT")
         nc.scalar.copy(out=eT[:], in_=eT_ps[:])
+
+        bT_ps = bank([P, 4, P], BF16, "bT_ps")
+        for j in range(4):
+            nc.tensor.transpose(bT_ps[:, j, :], biasrows[:, P * j : P * (j + 1)], ident_bf[:])
+        bcols = const.tile([P, 4, 4], F32, name="bcols")
+        nc.scalar.copy(out=bcols[:], in_=bT_ps[:, :, 0:4])
+        bhv = const.tile([P, 4], F32, name="bhv")
+        nc.gpsimd.tensor_tensor(out=bhv[:], in0=bcols[:, :, 2], in1=bcols[:, :, 3], op=ALU.add)
 
         def modulation(w, name):
             zT = bank([P, 4, P], F32, name)
@@ -112,44 +127,40 @@ def tile_graphditunit_pa_kernel(
 
         z_s = modulation(ws_sb, "z_s")
         z_g = modulation(wg_sb, "z_g")
-        bT_ps = bank([P, 4, P], BF16, "bT_ps")
-        for j in range(4):
-            nc.tensor.transpose(bT_ps[:, j, :], biasrows[:, P * j : P * (j + 1)], ident_bf[:])
-        warm_ps = bank([P, DO], F32, "warm_ps")
-        for n in range(WARM_MATMULS):
-            nc.tensor.matmul(out=warm_ps[:], lhsT=ident_bf[:], rhs=ws_sb[:], start=True, stop=True)
-        bcols = const.tile([P, 4, 4], F32, name="bcols")
-        nc.scalar.copy(out=bcols[:], in_=bT_ps[:, :, 0:4])
-        bhv = const.tile([P, 4], F32, name="bhv")
-        nc.gpsimd.tensor_tensor(out=bhv[:], in0=bcols[:, :, 2], in1=bcols[:, :, 3], op=ALU.add)
+        warm_up()
         sT = const.tile([P, 4, P], F32, name="sT")
         for j in range(4):
             nc.scalar.activation(out=sT[:, j, :], in_=z_s[:, j, :], func=ACT.Tanh, bias=bcols[:, j, 0:1])
         gT = const.tile([P, 4, P], F32, name="gT")
         for j in range(4):
             nc.scalar.activation(out=gT[:, j, :], in_=z_g[:, j, :], func=ACT.Sigmoid, bias=bcols[:, j, 1:2])
+
+        w_grp = []
+        for h in range(2):
+            wg = const.tile([P, DO // 2, 4], BF16, name="w_grp%d" % h, align_bytes=64)
+            nc.vector.tensor_copy(out=wg[:], in_=w_raw[h][:].rearrange("p j c -> p c j"))
+            w_grp.append(wg)
+        w_codes = const.tile([P, DO], U32, name="w_codes", align_bytes=64)
+        w_scales = const.tile([P, DO], U8, name="w_scales", align_bytes=64)
+        for h in range(2):
+            cols = slice(256 * h, 256 * (h + 1))
+            nc.vector.quantize_mx(
+                out=w_codes[:, cols].bitcast(FP8X4),
+                scales=w_scales[:, cols],
+                in_=w_grp[h][:].rearrange("p c j -> p (c j)"),
+            )
         sbv = const.tile([P, 4, P], F32, name="sbv")
         for j in range(4):
             nc.scalar.activation(
                 out=sbv[:, j, :], in_=sT[:, j, :], func=ACT.Identity, scale=bcols[:, j, 3:4], bias=bhv[:, j : j + 1]
             )
         z_h = modulation(wh_sb, "z_h")
-
-        w_grp = const.tile([P, DO, 4], BF16, name="w_grp", align_bytes=64)
-        for h in range(2):
-            nc.vector.tensor_copy(
-                out=w_grp[:, 256 * h : 256 * (h + 1), :], in_=w_raw[h][:].rearrange("p j c -> p c j")
-            )
-        w_codes = const.tile([P, DO], U32, name="w_codes", align_bytes=64)
-        w_scales = const.tile([P, DO], U8, name="w_scales", align_bytes=64)
-        nc.vector.quantize_mx(
-            out=w_codes[:].bitcast(FP8X4), scales=w_scales[:], in_=w_grp[:].rearrange("p c j -> p (c j)")
-        )
-
-        aT = const.tile([P, 4, P], F32, name="aT")
-        nc.vector.scalar_tensor_tensor(out=aT[:], in0=sT[:], scalar=1.0, in1=gT[:], op0=ALU.add, op1=ALU.mult)
+        x_transpose(0)
         u2 = const.tile([P, 4, P], F32, name="u2")
         nc.vector.tensor_tensor(out=u2[:], in0=z_h[:], in1=sbv[:], op=ALU.add)
+        x_quantise(0)
+        aT = const.tile([P, 4, P], F32, name="aT")
+        nc.vector.scalar_tensor_tensor(out=aT[:], in0=sT[:], scalar=1.0, in1=gT[:], op0=ALU.add, op1=ALU.mult)
         cT = const.tile([P, 4, P], F32, name="cT")
         nc.gpsimd.tensor_tensor(out=cT[:], in0=u2[:], in1=gT[:], op=ALU.mult)
 
@@ -258,17 +269,9 @@ def tile_graphditunit_pa_kernel(
                 out=facv[:, i : i + 1], in0=recv[:, i : i + 1], scalar1=448.0, scalar2=None, op0=ALU.mult
             )
 
-        def keep_warm():
-            nc.tensor.matmul(out=warm_ps[:, 0:P], lhsT=ident_f[:], rhs=ident_f[:], start=True, stop=True)
-
-        x_transpose(0)
-        x_quantise(0)
-        x_transpose(1)
-        x_quantise(1)
-        keep_warm()
-        for c in range(2, X_AHEAD):
+        for c in range(1, X_AHEAD):
             x_transpose(c)
-        keep_warm()
+        x_quantise(1)
         mx_pair(0)
 
         for k in range(n_pairs):

@@ -42,8 +42,6 @@ def tile_graphditunit_pa_kernel(
         nc.gpsimd.memset(zeros[:], 0.0)
         warm = const.tile([P, 1], F32, name="warm")
         nc.scalar.activation(out=warm[:], in_=zeros[:], func=ACT.Sigmoid)
-        ones = const.tile([P, DO], BF16, name="ones")
-        nc.vector.memset(ones[:].bitcast(U32), 0x3F803F80)
         biasrows = const.tile([P, DO], BF16, name="biasrows")
         nc.gpsimd.memset(biasrows[:].bitcast(U32), 0)
         ident_bf = const.tile([P, P], BF16, name="ident_bf")
@@ -99,13 +97,6 @@ def tile_graphditunit_pa_kernel(
             x_codes[c] = xc
             x_scales[c] = xs
 
-        warm_ps = bank([P, DO], F32, "warm_ps")
-
-        def warm_up():
-            nc.tensor.matmul(out=warm_ps[:], lhsT=ones[:, 0:P], rhs=ones[:], start=True, stop=True)
-
-        warm_up()
-        warm_up()
         eT_ps = bank([P, P], BF16, "eT_ps")
         nc.tensor.transpose(eT_ps[:], e_sb[:], ident_bf[:])
         eT = const.tile([P, P], BF16, name="eT")
@@ -127,6 +118,15 @@ def tile_graphditunit_pa_kernel(
 
         z_s = modulation(ws_sb, "z_s")
         z_g = modulation(wg_sb, "z_g")
+        warm_ps = bank([P, DO], F32, "warm_ps")
+
+        def warm_up():
+            nc.tensor.matmul(out=warm_ps[:], lhsT=ident_bf[:], rhs=ws_sb[:], start=True, stop=True)
+
+        def keep_warm():
+            nc.tensor.matmul(out=warm_ps[:, 0:P], lhsT=ident_f[:], rhs=ident_f[:], start=True, stop=True)
+
+        warm_up()
         warm_up()
         sT = const.tile([P, 4, P], F32, name="sT")
         for j in range(4):
@@ -155,14 +155,15 @@ def tile_graphditunit_pa_kernel(
                 out=sbv[:, j, :], in_=sT[:, j, :], func=ACT.Identity, scale=bcols[:, j, 3:4], bias=bhv[:, j : j + 1]
             )
         z_h = modulation(wh_sb, "z_h")
-        x_transpose(0)
-        u2 = const.tile([P, 4, P], F32, name="u2")
-        nc.vector.tensor_tensor(out=u2[:], in0=z_h[:], in1=sbv[:], op=ALU.add)
-        x_quantise(0)
+        warm_up()
         aT = const.tile([P, 4, P], F32, name="aT")
         nc.vector.scalar_tensor_tensor(out=aT[:], in0=sT[:], scalar=1.0, in1=gT[:], op0=ALU.add, op1=ALU.mult)
+        u2 = const.tile([P, 4, P], F32, name="u2")
+        nc.vector.tensor_tensor(out=u2[:], in0=z_h[:], in1=sbv[:], op=ALU.add)
+        x_transpose(0)
+        x_quantise(0)
         cT = const.tile([P, 4, P], F32, name="cT")
-        nc.gpsimd.tensor_tensor(out=cT[:], in0=u2[:], in1=gT[:], op=ALU.mult)
+        nc.vector.tensor_tensor(out=cT[:], in0=u2[:], in1=gT[:], op=ALU.mult)
 
         amax = const.tile([P, ROWS], F32, name="amax")
         rec = const.tile([P, ROWS], F32, name="rec")
@@ -269,9 +270,12 @@ def tile_graphditunit_pa_kernel(
                 out=facv[:, i : i + 1], in0=recv[:, i : i + 1], scalar1=448.0, scalar2=None, op0=ALU.mult
             )
 
-        for c in range(1, X_AHEAD):
-            x_transpose(c)
+        x_transpose(1)
+        keep_warm()
+        x_transpose(2)
         x_quantise(1)
+        x_transpose(3)
+        keep_warm()
         mx_pair(0)
 
         for k in range(n_pairs):

@@ -127,10 +127,14 @@ def tile_graphditunit_pa_kernel(
             nc.tensor.matmul(out=warm_ps[:, 0:P], lhsT=ident_f[:], rhs=ident_f[:], start=True, stop=True)
 
         warm_up()
-        warm_up()
         sT = const.tile([P, 4, P], F32, name="sT")
         for j in range(4):
             nc.scalar.activation(out=sT[:, j, :], in_=z_s[:, j, :], func=ACT.Tanh, bias=bcols[:, j, 0:1])
+        sbv = const.tile([P, 4, P], F32, name="sbv")
+        for j in range(4):
+            nc.scalar.activation(
+                out=sbv[:, j, :], in_=sT[:, j, :], func=ACT.Identity, scale=bcols[:, j, 3:4], bias=bhv[:, j : j + 1]
+            )
         gT = const.tile([P, 4, P], F32, name="gT")
         for j in range(4):
             nc.scalar.activation(out=gT[:, j, :], in_=z_g[:, j, :], func=ACT.Sigmoid, bias=bcols[:, j, 1:2])
@@ -149,17 +153,12 @@ def tile_graphditunit_pa_kernel(
                 scales=w_scales[:, cols],
                 in_=w_grp[h][:].rearrange("p c j -> p (c j)"),
             )
-        sbv = const.tile([P, 4, P], F32, name="sbv")
-        for j in range(4):
-            nc.scalar.activation(
-                out=sbv[:, j, :], in_=sT[:, j, :], func=ACT.Identity, scale=bcols[:, j, 3:4], bias=bhv[:, j : j + 1]
-            )
         z_h = modulation(wh_sb, "z_h")
         warm_up()
-        aT = const.tile([P, 4, P], F32, name="aT")
-        nc.vector.scalar_tensor_tensor(out=aT[:], in0=sT[:], scalar=1.0, in1=gT[:], op0=ALU.add, op1=ALU.mult)
         u2 = const.tile([P, 4, P], F32, name="u2")
         nc.vector.tensor_tensor(out=u2[:], in0=z_h[:], in1=sbv[:], op=ALU.add)
+        aT = const.tile([P, 4, P], F32, name="aT")
+        nc.vector.scalar_tensor_tensor(out=aT[:], in0=sT[:], scalar=1.0, in1=gT[:], op0=ALU.add, op1=ALU.mult)
         x_transpose(0)
         x_quantise(0)
         cT = const.tile([P, 4, P], F32, name="cT")
@@ -284,11 +283,11 @@ def tile_graphditunit_pa_kernel(
                 mx_pair(k + 1)
             times_a(2 * k)
             times_a(2 * k + 1)
+            turn_back(2 * k, last)
+            turn_back(2 * k + 1, last)
             if k >= 2:
                 cast_and_store(2 * k - 4, False, fac)
                 cast_and_store(2 * k - 3, False, fac)
-            turn_back(2 * k, last)
-            turn_back(2 * k + 1, last)
             if k + X_AHEAD < n_pairs:
                 x_transpose(k + X_AHEAD)
             if k + 2 < n_pairs:

@@ -44,6 +44,12 @@ def tile_graphditunit_pa_kernel(
         nc.scalar.activation(out=warm[:], in_=zeros[:], func=ACT.Sigmoid)
         biasrows = const.tile([P, DO], BF16, name="biasrows")
         nc.gpsimd.memset(biasrows[:].bitcast(U32), 0)
+        ramp = const.tile([P, P], F32, name="ramp")
+        nc.gpsimd.iota(
+            ramp[:], pattern=[[1, P]], base=1, channel_multiplier=1, allow_small_or_imprecise_dtypes=True
+        )
+        spin = const.tile([P, P], F32, name="spin")
+        nc.vector.tensor_scalar(out=spin[:], in0=ramp[:], scalar1=0.3183099, scalar2=None, op0=ALU.mult)
         ident_bf = const.tile([P, P], BF16, name="ident_bf")
         make_identity(nc, ident_bf[:])
         ident_f = const.tile([P, P], F32, name="ident_f")
@@ -57,13 +63,13 @@ def tile_graphditunit_pa_kernel(
         nc.sync.dma_start(out=ws_sb[:], in_=Wscale)
         for j, b in enumerate((bscale, bgate, bshift, bv)):
             nc.sync.dma_start(out=biasrows[j : j + 1, :], in_=b.rearrange("(o n) -> o n", o=1))
-        wg_sb = const.tile([P, DO], BF16, name="wg_sb")
-        nc.sync.dma_start(out=wg_sb[:], in_=Wgate)
         w_raw = []
         for h in range(2):
             wr = const.tile([P, 4, DO // 2], BF16, name="w_raw%d" % h)
             nc.sync.dma_start(out=wr[:], in_=Wv[:, 256 * h : 256 * (h + 1)].rearrange("(p j) c -> p j c", j=4))
             w_raw.append(wr)
+        wg_sb = const.tile([P, DO], BF16, name="wg_sb")
+        nc.sync.dma_start(out=wg_sb[:], in_=Wgate)
         wh_sb = const.tile([P, DO], BF16, name="wh_sb")
         nc.sync.dma_start(out=wh_sb[:], in_=Wshift)
         x_sb = []
@@ -97,6 +103,16 @@ def tile_graphditunit_pa_kernel(
             x_codes[c] = xc
             x_scales[c] = xs
 
+        def warm_up():
+            wk = bank([P, DO], F32, "wk")
+            nc.tensor.matmul(out=wk[:], lhsT=ident_bf[:], rhs=ws_sb[:], start=True, stop=True)
+
+        def keep_warm(src):
+            wk = bank([P, P], F32, "wk")
+            nc.tensor.matmul(out=wk[:], lhsT=src[:], rhs=src[:], start=True, stop=True)
+
+        for n in range(3):
+            keep_warm(spin)
         eT_ps = bank([P, P], BF16, "eT_ps")
         nc.tensor.transpose(eT_ps[:], e_sb[:], ident_bf[:])
         eT = const.tile([P, P], BF16, name="eT")
@@ -117,24 +133,11 @@ def tile_graphditunit_pa_kernel(
             return zT
 
         z_s = modulation(ws_sb, "z_s")
-        z_g = modulation(wg_sb, "z_g")
-        warm_ps = bank([P, DO], F32, "warm_ps")
-
-        def warm_up():
-            nc.tensor.matmul(out=warm_ps[:], lhsT=ident_bf[:], rhs=ws_sb[:], start=True, stop=True)
-
-        def keep_warm():
-            nc.tensor.matmul(out=warm_ps[:, 0:P], lhsT=ident_f[:], rhs=ident_f[:], start=True, stop=True)
-
         warm_up()
+        z_g = modulation(wg_sb, "z_g")
         sT = const.tile([P, 4, P], F32, name="sT")
         for j in range(4):
             nc.scalar.activation(out=sT[:, j, :], in_=z_s[:, j, :], func=ACT.Tanh, bias=bcols[:, j, 0:1])
-        sbv = const.tile([P, 4, P], F32, name="sbv")
-        for j in range(4):
-            nc.scalar.activation(
-                out=sbv[:, j, :], in_=sT[:, j, :], func=ACT.Identity, scale=bcols[:, j, 3:4], bias=bhv[:, j : j + 1]
-            )
         gT = const.tile([P, 4, P], F32, name="gT")
         for j in range(4):
             nc.scalar.activation(out=gT[:, j, :], in_=z_g[:, j, :], func=ACT.Sigmoid, bias=bcols[:, j, 1:2])
@@ -152,6 +155,16 @@ def tile_graphditunit_pa_kernel(
                 out=w_codes[:, cols].bitcast(FP8X4),
                 scales=w_scales[:, cols],
                 in_=w_grp[h][:].rearrange("p c j -> p (c j)"),
+            )
+        sbv = const.tile([P, 4, P], F32, name="sbv")
+        for j in range(4):
+            nc.vector.tensor_scalar(
+                out=sbv[:, j, :],
+                in0=sT[:, j, :],
+                scalar1=bcols[:, j, 3:4],
+                scalar2=bhv[:, j : j + 1],
+                op0=ALU.mult,
+                op1=ALU.add,
             )
         z_h = modulation(wh_sb, "z_h")
         warm_up()
@@ -270,11 +283,11 @@ def tile_graphditunit_pa_kernel(
             )
 
         x_transpose(1)
-        keep_warm()
+        keep_warm(ident_f)
         x_transpose(2)
         x_quantise(1)
         x_transpose(3)
-        keep_warm()
+        keep_warm(ident_f)
         mx_pair(0)
 
         for k in range(n_pairs):
@@ -299,5 +312,5 @@ def tile_graphditunit_pa_kernel(
         row_factor_tile(ROWS - 2)
         cast_and_store(ROWS - 3, False, fac)
         row_factor_tile(ROWS - 1)
-        cast_and_store(ROWS - 2, False, facv)
+        cast_and_store(ROWS - 2, True, facv)
         cast_and_store(ROWS - 1, True, facv)

@@ -20,6 +20,7 @@ DO = 512
 FLOPS = 2 * 2048 * 512 * 512 + 3 * 2 * 128 * 128 * 512
 
 X_AHEAD = 4
+DIRECT = (5, 7, 9, 11, 13, 15)
 STORE_GROUPS = ((0, 4), (4, 4), (8, 4), (12, 2), (14, 2))
 
 
@@ -39,17 +40,15 @@ def tile_graphditunit_pa_kernel(
             return psum.tile(shape, dtype, name=name, tag="bank", bufs=8)
 
         zeros = const.tile([P, 1], F32, name="zeros")
-        nc.gpsimd.memset(zeros[:], 0.0)
+        nc.vector.memset(zeros[:], 0.0)
         warm = const.tile([P, 1], F32, name="warm")
         nc.scalar.activation(out=warm[:], in_=zeros[:], func=ACT.Sigmoid)
         biasrows = const.tile([P, DO], BF16, name="biasrows")
-        nc.gpsimd.memset(biasrows[:].bitcast(U32), 0)
+        nc.vector.memset(biasrows[:].bitcast(U32), 0)
         ramp = const.tile([P, P], F32, name="ramp")
         nc.gpsimd.iota(
             ramp[:], pattern=[[1, P]], base=1, channel_multiplier=1, allow_small_or_imprecise_dtypes=True
         )
-        spin = const.tile([P, P], F32, name="spin")
-        nc.vector.tensor_scalar(out=spin[:], in0=ramp[:], scalar1=0.3183099, scalar2=None, op0=ALU.mult)
         ident_bf = const.tile([P, P], BF16, name="ident_bf")
         make_identity(nc, ident_bf[:])
         ident_f = const.tile([P, P], F32, name="ident_f")
@@ -111,8 +110,8 @@ def tile_graphditunit_pa_kernel(
             wk = bank([P, P], F32, "wk")
             nc.tensor.matmul(out=wk[:], lhsT=src[:], rhs=src[:], start=True, stop=True)
 
-        for n in range(3):
-            keep_warm(spin)
+        for n in range(2):
+            keep_warm(ramp)
         eT_ps = bank([P, P], BF16, "eT_ps")
         nc.tensor.transpose(eT_ps[:], e_sb[:], ident_bf[:])
         eT = const.tile([P, P], BF16, name="eT")
@@ -186,6 +185,7 @@ def tile_graphditunit_pa_kernel(
         o_tiles = {}
         p_tiles = {}
         q_tiles = {}
+        a_rows = []
         group_of = {}
         for first, count in STORE_GROUPS:
             for i in range(first, first + count):
@@ -218,32 +218,53 @@ def tile_graphditunit_pa_kernel(
             if i == first + count - 1:
                 nc.sync.dma_start(out=out_1[:, first : first + count, :], in_=qt[:].bitcast(U8))
 
-        def mx_pair(c):
-            for t in range(2):
-                accT = bank([P, 4, P], F32, "accT")
-                acc_tiles[2 * c + t] = accT
-                rows = slice(P * t, P * (t + 1))
-                for j in range(4):
-                    cols = slice(P * j, P * (j + 1))
-                    nc.tensor.matmul_mx(
-                        out=accT[:, j, :],
-                        lhsT=w_codes[:, cols].bitcast(FP8X4),
-                        lhsT_scale=w_scales[:, cols],
-                        rhs=x_codes[c][:, rows].bitcast(FP8X4),
-                        rhs_scale=x_scales[c][:, rows],
-                        start=True,
-                        stop=True,
-                    )
+        def mx_tile(i):
+            c, t = divmod(i, 2)
+            rows = slice(P * t, P * (t + 1))
+            if i in DIRECT:
+                acc = bank([P, DO], F32, "acc")
+                nc.tensor.matmul_mx(
+                    out=acc[:],
+                    lhsT=x_codes[c][:, rows].bitcast(FP8X4),
+                    lhsT_scale=x_scales[c][:, rows],
+                    rhs=w_codes[:].bitcast(FP8X4),
+                    rhs_scale=w_scales[:],
+                    start=True,
+                    stop=True,
+                )
+                acc_tiles[i] = acc
+                return
+            accT = bank([P, 4, P], F32, "accT")
+            acc_tiles[i] = accT
+            for j in range(4):
+                cols = slice(P * j, P * (j + 1))
+                nc.tensor.matmul_mx(
+                    out=accT[:, j, :],
+                    lhsT=w_codes[:, cols].bitcast(FP8X4),
+                    lhsT_scale=w_scales[:, cols],
+                    rhs=x_codes[c][:, rows].bitcast(FP8X4),
+                    rhs_scale=x_scales[c][:, rows],
+                    start=True,
+                    stop=True,
+                )
+
+        def out_tile(i):
+            if i // 2 not in o_tiles:
+                o_tiles[i // 2] = work.tile([P, 2, DO], F32, name="o", tag="o", bufs=5)
+            return o_tiles[i // 2]
 
         def times_a(i):
+            if i in DIRECT:
+                prod = work.tile([P, DO], F32, name="prod", tag="prod", bufs=2)
+                nc.vector.tensor_tensor(out=prod[:], in0=acc_tiles[i][:], in1=a_rows[0][:], op=ALU.mult)
+                p_tiles[i] = prod
+                return
             prodT = work.tile([P, 4, P], F32, name="prodT", tag="prodT", bufs=4)
             p_tiles[i] = prodT
             nc.vector.tensor_tensor(out=prodT[:], in0=acc_tiles[i][:], in1=aT[:], op=ALU.mult)
 
-        def turn_back(i, store_now):
-            if i % 2 == 0:
-                o_tiles[i // 2] = work.tile([P, 2, DO], F32, name="o", tag="o", bufs=5)
-            o = o_tiles[i // 2]
+        def turn_back(i):
+            o = out_tile(i)
             o_ps = bank([P, DO], F32, "o_ps")
             for j in range(4):
                 cols = slice(P * j, P * (j + 1))
@@ -254,10 +275,23 @@ def tile_graphditunit_pa_kernel(
                     out=o_ps[:, cols], lhsT=p_tiles[i][:, j, :], rhs=ident_f[:], start=False, stop=True, is_transpose=True
                 )
             nc.scalar.copy(out=o[:, i % 2, :], in_=o_ps[:])
-            if store_now:
-                nc.sync.dma_start(out=out_0[:, i : i + 1, :], in_=o[:, i % 2 : i % 2 + 1, :])
-            elif i % 2 == 1:
-                nc.sync.dma_start(out=out_0[:, i - 1 : i + 1, :], in_=o[:])
+
+        def add_c(i, engine):
+            engine.tensor_tensor(out=out_tile(i)[:, i % 2, :], in0=p_tiles[i][:], in1=a_rows[1][:], op=ALU.add)
+
+        def rows_layout(src, name):
+            ps = bank([P, DO], F32, name + "_ps")
+            for j in range(4):
+                nc.tensor.transpose(ps[:, P * j : P * (j + 1)], src[:, j, :], ident_f[:])
+            dst = const.tile([P, DO], F32, name=name)
+            nc.scalar.copy(out=dst[:], in_=ps[:])
+            a_rows.append(dst)
+
+        def store_pair(c):
+            nc.sync.dma_start(out=out_0[:, 2 * c : 2 * c + 2, :], in_=o_tiles[c][:])
+
+        def store_tile(i):
+            nc.sync.dma_start(out=out_0[:, i : i + 1, :], in_=o_tiles[i // 2][:, i % 2 : i % 2 + 1, :])
 
         def row_factors_pair(c):
             cols = slice(2 * c, 2 * c + 2)
@@ -269,7 +303,7 @@ def tile_graphditunit_pa_kernel(
                 out=fac[:, cols], in0=rec[:, cols], scalar1=448.0, scalar2=0.0, op0=ALU.mult, op1=ALU.add
             )
 
-        def row_factor_tile(i):
+        def row_max_tile(i):
             nc.vector.tensor_reduce(
                 out=amax[:, i : i + 1],
                 in_=o_tiles[i // 2][:, i % 2, :],
@@ -277,10 +311,11 @@ def tile_graphditunit_pa_kernel(
                 op=ALU.max,
                 apply_absolute_value=True,
             )
-            nc.vector.reciprocal(out=recv[:, i : i + 1], in_=amax[:, i : i + 1])
-            nc.vector.tensor_scalar(
-                out=facv[:, i : i + 1], in0=recv[:, i : i + 1], scalar1=448.0, scalar2=None, op0=ALU.mult
-            )
+
+        def last_factors():
+            cols = slice(ROWS - 2, ROWS)
+            nc.vector.reciprocal(out=recv[:, cols], in_=amax[:, cols])
+            nc.vector.tensor_scalar(out=facv[:, cols], in0=recv[:, cols], scalar1=448.0, scalar2=None, op0=ALU.mult)
 
         x_transpose(1)
         keep_warm(ident_f)
@@ -288,29 +323,44 @@ def tile_graphditunit_pa_kernel(
         x_quantise(1)
         x_transpose(3)
         keep_warm(ident_f)
-        mx_pair(0)
+        mx_tile(0)
+        mx_tile(1)
 
         for k in range(n_pairs):
+            pair = (2 * k, 2 * k + 1)
             last = k == n_pairs - 1
             if not last:
-                mx_pair(k + 1)
-            times_a(2 * k)
-            times_a(2 * k + 1)
-            turn_back(2 * k, last)
-            turn_back(2 * k + 1, last)
+                mx_tile(2 * k + 2)
+                mx_tile(2 * k + 3)
+            for i in pair:
+                times_a(i)
+            if k + 2 < n_pairs:
+                x_quantise(k + 2)
+            for i in pair:
+                if i in DIRECT:
+                    add_c(i, nc.gpsimd)
+                else:
+                    turn_back(i)
+                if last:
+                    store_tile(i)
+            if not last:
+                store_pair(k)
+            if k == 0:
+                rows_layout(aT, "a_row")
+            if k == 1:
+                rows_layout(cT, "c_row")
             if k >= 2:
                 cast_and_store(2 * k - 4, False, fac)
                 cast_and_store(2 * k - 3, False, fac)
             if k + X_AHEAD < n_pairs:
                 x_transpose(k + X_AHEAD)
-            if k + 2 < n_pairs:
-                x_quantise(k + 2)
             if k >= 1:
                 row_factors_pair(k - 1)
 
         cast_and_store(ROWS - 4, False, fac)
-        row_factor_tile(ROWS - 2)
         cast_and_store(ROWS - 3, False, fac)
-        row_factor_tile(ROWS - 1)
+        row_max_tile(ROWS - 2)
+        row_max_tile(ROWS - 1)
+        last_factors()
         cast_and_store(ROWS - 2, True, facv)
         cast_and_store(ROWS - 1, True, facv)

@@ -20,6 +20,7 @@ DO = 512
 FLOPS = 2 * 2048 * 512 * 512 + 3 * 2 * 128 * 128 * 512
 
 X_AHEAD = 4
+SPLIT_PAIRS = 8
 DIRECT = (5, 7, 9, 11, 13, 15)
 STORE_GROUPS = ((0, 4), (4, 4), (8, 4), (12, 2), (14, 2))
 
@@ -293,15 +294,22 @@ def tile_graphditunit_pa_kernel(
         def store_tile(i):
             nc.sync.dma_start(out=out_0[:, i : i + 1, :], in_=o_tiles[i // 2][:, i % 2 : i % 2 + 1, :])
 
-        def row_factors_pair(c):
+        def times_448(c):
             cols = slice(2 * c, 2 * c + 2)
-            nc.vector.tensor_reduce(
-                out=amax[:, cols], in_=o_tiles[c][:], axis=AX.X, op=ALU.max, apply_absolute_value=True
-            )
+            nc.scalar.activation(out=fac[:, cols], in_=rec[:, cols], func=ACT.Copy, scale=448.0)
+
+        def row_factors_pair(c, on_vector):
+            cols = slice(2 * c, 2 * c + 2)
+            if c < SPLIT_PAIRS:
+                row_max_tile(2 * c)
+                row_max_tile(2 * c + 1)
+            else:
+                nc.vector.tensor_reduce(
+                    out=amax[:, cols], in_=o_tiles[c][:], axis=AX.X, op=ALU.max, apply_absolute_value=True
+                )
+            if on_vector:
+                return
             nc.gpsimd.tensor_tensor(out=rec[:, cols], in0=amax[:, cols], in1=minus_one[:, cols], op=ALU.pow)
-            nc.gpsimd.tensor_scalar(
-                out=fac[:, cols], in0=rec[:, cols], scalar1=448.0, scalar2=0.0, op0=ALU.mult, op1=ALU.add
-            )
 
         def row_max_tile(i):
             nc.vector.tensor_reduce(
@@ -312,8 +320,8 @@ def tile_graphditunit_pa_kernel(
                 apply_absolute_value=True,
             )
 
-        def last_factors():
-            cols = slice(ROWS - 2, ROWS)
+        def vector_factors(c):
+            cols = slice(2 * c, 2 * c + 2)
             nc.vector.reciprocal(out=recv[:, cols], in_=amax[:, cols])
             nc.vector.tensor_scalar(out=facv[:, cols], in0=recv[:, cols], scalar1=448.0, scalar2=None, op0=ALU.mult)
 
@@ -336,6 +344,8 @@ def tile_graphditunit_pa_kernel(
                 times_a(i)
             if k + 2 < n_pairs:
                 x_quantise(k + 2)
+            if k >= 2:
+                times_448(k - 2)
             for i in pair:
                 if i in DIRECT:
                     add_c(i, nc.gpsimd)
@@ -355,12 +365,13 @@ def tile_graphditunit_pa_kernel(
             if k + X_AHEAD < n_pairs:
                 x_transpose(k + X_AHEAD)
             if k >= 1:
-                row_factors_pair(k - 1)
+                row_factors_pair(k - 1, last)
 
-        cast_and_store(ROWS - 4, False, fac)
-        cast_and_store(ROWS - 3, False, fac)
         row_max_tile(ROWS - 2)
+        vector_factors(n_pairs - 2)
+        cast_and_store(ROWS - 4, False, facv)
+        cast_and_store(ROWS - 3, False, facv)
         row_max_tile(ROWS - 1)
-        last_factors()
+        vector_factors(n_pairs - 1)
         cast_and_store(ROWS - 2, True, facv)
         cast_and_store(ROWS - 1, True, facv)

from contextlib import ExitStack

import concourse.mybir as mybir
from concourse.masks import make_identity

F32 = mybir.dt.float32
BF16 = mybir.dt.bfloat16
U32 = mybir.dt.uint32
U8 = mybir.dt.uint8
FP8X4 = mybir.dt.float8_e4m3fn_x4
FP8 = mybir.dt.float8_e4m3fn
ALU = mybir.AluOpType
ACT = mybir.ActivationFunctionType
AX = mybir.AxisListType

P = 128
ROWS = 16
D = 512
DO = 512
FLOPS = 2 * 2048 * 512 * 512 + 3 * 2 * 128 * 128 * 512

X_AHEAD = 4
SPLIT_PAIRS = 8
DIRECT = (5, 7, 9, 11, 13, 15)
STORE_GROUPS = ((0, 4), (4, 4), (8, 4), (12, 2), (14, 2))


def tile_graphditunit_pa_kernel(
    tc, x, edge_features, Wv, bv, Wgate, bgate, Wscale, bscale, Wshift, bshift, out_0, out_1
):
    nc = tc.nc
    n_pairs = ROWS // 2

    with ExitStack() as ctx:
        const = ctx.enter_context(tc.tile_pool(name="const", bufs=1))
        work = ctx.enter_context(tc.tile_pool(name="work", bufs=3))
        psum = ctx.enter_context(tc.psum_pool(name="psum", bufs=8))
        ctx.enter_context(tc.manual_schedule())

        def bank(shape, dtype, name):
            return psum.tile(shape, dtype, name=name, tag="bank", bufs=8)

        zeros = const.tile([P, 1], F32, name="zeros")
        nc.vector.memset(zeros[:], 0.0)
        warm = const.tile([P, 1], F32, name="warm")
        nc.scalar.activation(out=warm[:], in_=zeros[:], func=ACT.Sigmoid)
        biasrows = const.tile([P, DO], BF16, name="biasrows")
        nc.vector.memset(biasrows[:].bitcast(U32), 0)
        ramp = const.tile([P, P], F32, name="ramp")
        nc.gpsimd.iota(
            ramp[:], pattern=[[1, P]], base=1, channel_multiplier=1, allow_small_or_imprecise_dtypes=True
        )
        ident_bf = const.tile([P, P], BF16, name="ident_bf")
        make_identity(nc, ident_bf[:])
        ident_f = const.tile([P, P], F32, name="ident_f")
        make_identity(nc, ident_f[:])
        minus_one = const.tile([P, ROWS], F32, name="minus_one")
        nc.gpsimd.memset(minus_one[:], -1.0)

        e_sb = const.tile([P, P], BF16, name="e_sb")
        nc.sync.dma_start(out=e_sb[:], in_=edge_features)
        ws_sb = const.tile([P, DO], BF16, name="ws_sb")
        nc.sync.dma_start(out=ws_sb[:], in_=Wscale)
        for j, b in enumerate((bscale, bgate, bshift, bv)):
            nc.sync.dma_start(out=biasrows[j : j + 1, :], in_=b.rearrange("(o n) -> o n", o=1))
        w_raw = []
        for h in range(2):
            wr = const.tile([P, 4, DO // 2], BF16, name="w_raw%d" % h)
            nc.sync.dma_start(out=wr[:], in_=Wv[:, 256 * h : 256 * (h + 1)].rearrange("(p j) c -> p j c", j=4))
            w_raw.append(wr)
        wg_sb = const.tile([P, DO], BF16, name="wg_sb")
        nc.sync.dma_start(out=wg_sb[:], in_=Wgate)
        wh_sb = const.tile([P, DO], BF16, name="wh_sb")
        nc.sync.dma_start(out=wh_sb[:], in_=Wshift)
        x_sb = []
        for c in range(n_pairs):
            x_sb.append(const.tile([P, 2, D], BF16, name="x_sb%d" % c))
        for c in range(n_pairs):
            nc.sync.dma_start(out=x_sb[c][:], in_=x[:, 2 * c : 2 * c + 2, :])

        x_codes = {}
        x_scales = {}
        xg_tiles = {}

        def x_transpose(c):
            words = x_sb[c][:].rearrange("p t k -> p (t k)").bitcast(F32)
            xt = bank([P, 2, 2, P], F32, "xt")
            for t in range(2):
                for u in range(2):
                    nc.tensor.transpose(xt[:, t, u, :], words[:, 256 * t + u : 256 * (t + 1) : 2], ident_f[:])
            xg = work.tile([P, 2, P, 2], F32, name="xg", tag="xg", bufs=8, align_bytes=64)
            nc.scalar.copy(out=xg[:], in_=xt[:].rearrange("p t u r -> p t r u"))
            xg_tiles[c] = xg

        def x_quantise(c):
            xc = const.tile([P, 2 * P], U32, name="xc%d" % c, align_bytes=64)
            xs = const.tile([P, 2 * P], U8, name="xs%d" % c, align_bytes=64)
            nc.vector.quantize_mx(
                out=xc[:].bitcast(FP8X4),
                scales=xs[:],
                in_=xg_tiles[c][:].rearrange("p t r u -> p (t r u)").bitcast(BF16),
            )
            x_codes[c] = xc
            x_scales[c] = xs

        def warm_up():
            wk = bank([P, DO], F32, "wk")
            nc.tensor.matmul(out=wk[:], lhsT=ident_bf[:], rhs=ws_sb[:], start=True, stop=True)

        def keep_warm(src):
            wk = bank([P, P], F32, "wk")
            nc.tensor.matmul(out=wk[:], lhsT=src[:], rhs=src[:], start=True, stop=True)

        for n in range(2):
            keep_warm(ramp)
        eT_ps = bank([P, P], BF16, "eT_ps")
        nc.tensor.transpose(eT_ps[:], e_sb[:], ident_bf[:])
        eT = const.tile([P, P], BF16, name="eT")
        nc.scalar.copy(out=eT[:], in_=eT_ps[:])

        bT_ps = bank([P, 4, P], BF16, "bT_ps")
        for j in range(4):
            nc.tensor.transpose(bT_ps[:, j, :], biasrows[:, P * j : P * (j + 1)], ident_bf[:])
        bcols = const.tile([P, 4, 4], F32, name="bcols")
        nc.scalar.copy(out=bcols[:], in_=bT_ps[:, :, 0:4])
        bhv = const.tile([P, 4], F32, name="bhv")
        nc.gpsimd.tensor_tensor(out=bhv[:], in0=bcols[:, :, 2], in1=bcols[:, :, 3], op=ALU.add)

        def modulation(w, name):
            zT = bank([P, 4, P], F32, name)
            for j in range(4):
                nc.tensor.matmul(out=zT[:, j, :], lhsT=w[:, P * j : P * (j + 1)], rhs=eT[:], start=True, stop=True)
            return zT

        z_s = modulation(ws_sb, "z_s")
        warm_up()
        z_g = modulation(wg_sb, "z_g")
        sT = const.tile([P, 4, P], F32, name="sT")
        for j in range(4):
            nc.scalar.activation(out=sT[:, j, :], in_=z_s[:, j, :], func=ACT.Tanh, bias=bcols[:, j, 0:1])
        gT = const.tile([P, 4, P], F32, name="gT")
        for j in range(4):
            nc.scalar.activation(out=gT[:, j, :], in_=z_g[:, j, :], func=ACT.Sigmoid, bias=bcols[:, j, 1:2])

        w_grp = []
        for h in range(2):
            wg = const.tile([P, DO // 2, 4], BF16, name="w_grp%d" % h, align_bytes=64)
            nc.vector.tensor_copy(out=wg[:], in_=w_raw[h][:].rearrange("p j c -> p c j"))
            w_grp.append(wg)
        w_codes = const.tile([P, DO], U32, name="w_codes", align_bytes=64)
        w_scales = const.tile([P, DO], U8, name="w_scales", align_bytes=64)
        for h in range(2):
            cols = slice(256 * h, 256 * (h + 1))
            nc.vector.quantize_mx(
                out=w_codes[:, cols].bitcast(FP8X4),
                scales=w_scales[:, cols],
                in_=w_grp[h][:].rearrange("p c j -> p (c j)"),
            )
        sbv = const.tile([P, 4, P], F32, name="sbv")
        for j in range(4):
            nc.vector.tensor_scalar(
                out=sbv[:, j, :],
                in0=sT[:, j, :],
                scalar1=bcols[:, j, 3:4],
                scalar2=bhv[:, j : j + 1],
                op0=ALU.mult,
                op1=ALU.add,
            )
        z_h = modulation(wh_sb, "z_h")
        warm_up()
        u2 = const.tile([P, 4, P], F32, name="u2")
        nc.vector.tensor_tensor(out=u2[:], in0=z_h[:], in1=sbv[:], op=ALU.add)
        aT = const.tile([P, 4, P], F32, name="aT")
        nc.vector.scalar_tensor_tensor(out=aT[:], in0=sT[:], scalar=1.0, in1=gT[:], op0=ALU.add, op1=ALU.mult)
        x_transpose(0)
        x_quantise(0)
        cT = const.tile([P, 4, P], F32, name="cT")
        nc.vector.tensor_tensor(out=cT[:], in0=u2[:], in1=gT[:], op=ALU.mult)

        amax = const.tile([P, ROWS], F32, name="amax")
        rec = const.tile([P, ROWS], F32, name="rec")
        recv = const.tile([P, ROWS], F32, name="recv")
        fac = const.tile([P, ROWS], F32, name="fac")
        facv = const.tile([P, ROWS], F32, name="facv")
        acc_tiles = {}
        o_tiles = {}
        p_tiles = {}
        q_tiles = {}
        a_rows = []
        group_of = {}
        for first, count in STORE_GROUPS:
            for i in range(first, first + count):
                group_of[i] = (first, count)

        def cast_and_store(i, on_vector, factor):
            first, count = group_of[i]
            if i == first:
                q_tiles[first] = work.tile([P, count, DO], FP8, name="q", tag="q", bufs=3)
            qt = q_tiles[first]
            src = o_tiles[i // 2][:, i % 2, :]
            if on_vector:
                nc.vector.tensor_scalar(
                    out=qt[:, i - first, :],
                    in0=src,
                    scalar1=factor[:, i : i + 1],
                    scalar2=None,
                    op0=ALU.mult,
                    saturate=False,
                )
            else:
                nc.scalar.activation(
                    out=qt[:, i - first, :],
                    in_=src,
                    func=ACT.Identity,
                    bias=zeros[:, 0:1],
                    scale=factor[:, i : i + 1],
                    saturate=False,
                )
            if i == first + count - 1:
                nc.sync.dma_start(out=out_1[:, first : first + count, :], in_=qt[:].bitcast(U8))

        def mx_tile(i):
            c, t = divmod(i, 2)
            rows = slice(P * t, P * (t + 1))
            if i in DIRECT:
                acc = bank([P, DO], F32, "acc")
                nc.tensor.matmul_mx(
                    out=acc[:],
                    lhsT=x_codes[c][:, rows].bitcast(FP8X4),
                    lhsT_scale=x_scales[c][:, rows],
                    rhs=w_codes[:].bitcast(FP8X4),
                    rhs_scale=w_scales[:],
                    start=True,
                    stop=True,
                )
                acc_tiles[i] = acc
                return
            accT = bank([P, 4, P], F32, "accT")
            acc_tiles[i] = accT
            for j in range(4):
                cols = slice(P * j, P * (j + 1))
                nc.tensor.matmul_mx(
                    out=accT[:, j, :],
                    lhsT=w_codes[:, cols].bitcast(FP8X4),
                    lhsT_scale=w_scales[:, cols],
                    rhs=x_codes[c][:, rows].bitcast(FP8X4),
                    rhs_scale=x_scales[c][:, rows],
                    start=True,
                    stop=True,
                )

        def out_tile(i):
            if i // 2 not in o_tiles:
                o_tiles[i // 2] = work.tile([P, 2, DO], F32, name="o", tag="o", bufs=5)
            return o_tiles[i // 2]

        def times_a(i):
            if i in DIRECT:
                prod = work.tile([P, DO], F32, name="prod", tag="prod", bufs=2)
                nc.vector.tensor_tensor(out=prod[:], in0=acc_tiles[i][:], in1=a_rows[0][:], op=ALU.mult)
                p_tiles[i] = prod
                return
            prodT = work.tile([P, 4, P], F32, name="prodT", tag="prodT", bufs=4)
            p_tiles[i] = prodT
            nc.vector.tensor_tensor(out=prodT[:], in0=acc_tiles[i][:], in1=aT[:], op=ALU.mult)

        def turn_back(i):
            o = out_tile(i)
            o_ps = bank([P, DO], F32, "o_ps")
            for j in range(4):
                cols = slice(P * j, P * (j + 1))
                nc.tensor.matmul(
                    out=o_ps[:, cols], lhsT=cT[:, j, :], rhs=ident_f[:], start=True, stop=False, is_transpose=True
                )
                nc.tensor.matmul(
                    out=o_ps[:, cols], lhsT=p_tiles[i][:, j, :], rhs=ident_f[:], start=False, stop=True, is_transpose=True
                )
            nc.scalar.copy(out=o[:, i % 2, :], in_=o_ps[:])

        def add_c(i, engine):
            engine.tensor_tensor(out=out_tile(i)[:, i % 2, :], in0=p_tiles[i][:], in1=a_rows[1][:], op=ALU.add)

        def rows_layout(src, name):
            ps = bank([P, DO], F32, name + "_ps")
            for j in range(4):
                nc.tensor.transpose(ps[:, P * j : P * (j + 1)], src[:, j, :], ident_f[:])
            dst = const.tile([P, DO], F32, name=name)
            nc.scalar.copy(out=dst[:], in_=ps[:])
            a_rows.append(dst)

        def store_pair(c):
            nc.sync.dma_start(out=out_0[:, 2 * c : 2 * c + 2, :], in_=o_tiles[c][:])

        def store_tile(i):
            nc.sync.dma_start(out=out_0[:, i : i + 1, :], in_=o_tiles[i // 2][:, i % 2 : i % 2 + 1, :])

        def times_448(c):
            cols = slice(2 * c, 2 * c + 2)
            nc.scalar.activation(out=fac[:, cols], in_=rec[:, cols], func=ACT.Copy, scale=448.0)

        def row_factors_pair(c, on_vector):
            cols = slice(2 * c, 2 * c + 2)
            if c < SPLIT_PAIRS:
                row_max_tile(2 * c)
                row_max_tile(2 * c + 1)
            else:
                nc.vector.tensor_reduce(
                    out=amax[:, cols], in_=o_tiles[c][:], axis=AX.X, op=ALU.max, apply_absolute_value=True
                )
            if on_vector:
                return
            nc.gpsimd.tensor_tensor(out=rec[:, cols], in0=amax[:, cols], in1=minus_one[:, cols], op=ALU.pow)

        def row_max_tile(i):
            nc.vector.tensor_reduce(
                out=amax[:, i : i + 1],
                in_=o_tiles[i // 2][:, i % 2, :],
                axis=AX.X,
                op=ALU.max,
                apply_absolute_value=True,
            )

        def vector_factors(c):
            cols = slice(2 * c, 2 * c + 2)
            nc.vector.reciprocal(out=recv[:, cols], in_=amax[:, cols])
            nc.vector.tensor_scalar(out=facv[:, cols], in0=recv[:, cols], scalar1=448.0, scalar2=None, op0=ALU.mult)

        x_transpose(1)
        keep_warm(ident_f)
        x_transpose(2)
        x_quantise(1)
        x_transpose(3)
        keep_warm(ident_f)
        mx_tile(0)
        mx_tile(1)

        for k in range(n_pairs):
            pair = (2 * k, 2 * k + 1)
            last = k == n_pairs - 1
            if not last:
                mx_tile(2 * k + 2)
                mx_tile(2 * k + 3)
            for i in pair:
                times_a(i)
            if k + 2 < n_pairs:
                x_quantise(k + 2)
            if k >= 2:
                times_448(k - 2)
            for i in pair:
                if i in DIRECT:
                    add_c(i, nc.gpsimd)
                else:
                    turn_back(i)
                if last:
                    store_tile(i)
            if not last:
                store_pair(k)
            if k == 0:
                rows_layout(aT, "a_row")
            if k == 1:
                rows_layout(cT, "c_row")
            if k >= 2:
                cast_and_store(2 * k - 4, False, fac)
                cast_and_store(2 * k - 3, False, fac)
            if k + X_AHEAD < n_pairs:
                x_transpose(k + X_AHEAD)
            if k >= 1:
                row_factors_pair(k - 1, last)

        row_max_tile(ROWS - 2)
        vector_factors(n_pairs - 2)
        cast_and_store(ROWS - 4, False, facv)
        cast_and_store(ROWS - 3, False, facv)
        row_max_tile(ROWS - 1)
        vector_factors(n_pairs - 1)
        cast_and_store(ROWS - 2, True, facv)
        cast_and_store(ROWS - 1, True, facv)
